import numpy as np
import ml_dtypes


def mxq(x, axis, fmt="e4m3"):
    dtype, down = {"e4m3": (ml_dtypes.float8_e4m3fn, 7), "e5m2": (ml_dtypes.float8_e5m2, 14)}[fmt]
    v = np.moveaxis(np.asarray(x, np.float32).astype(ml_dtypes.bfloat16).astype(np.float64), axis, -1)
    blocks = v.reshape(v.shape[:-1] + (-1, 32))
    amax = np.abs(blocks).max(-1, keepdims=True)
    byte = np.maximum(np.where(amax > 0, np.frexp(amax)[1] - 1 + 127, 0) - down, 1)
    scale = np.exp2(byte - 127.0)
    codes = (blocks / scale).astype(np.float32).astype(dtype).astype(np.float64)
    return np.moveaxis((codes * scale).reshape(v.shape), -1, axis)


WIDE = False


def mx_kscale(k):
    if not WIDE:
        return np.ones(k)
    levels = np.array([10, -10, 5, -5, 0])
    a = np.random.permutation(np.resize(levels, k // 512 * 4)).reshape(k // 512, 4)
    idx = np.arange(k)
    return np.exp2(a[idx // 512, idx % 128 // 32])


BF16 = ml_dtypes.bfloat16


def bf(x):
    return np.asarray(x, np.float32).astype(BF16)


def f64(x):
    return np.asarray(x).astype(np.float64)


B, T, C, F = 4, 128, 512, 16384
M = T


def silu(v):
    return v / (1.0 + np.exp(-v))


def sigmoid(v):
    return 1.0 / (1.0 + np.exp(-v))


def setup_inputs():
    t = mx_kscale(F)
    x = np.random.standard_normal((B, T, C)) + 0.5 * np.random.standard_normal((B, 1, C))
    return {"h": bf(silu(np.random.standard_normal((B, T, F)) * 0.85) * t),
            "x": bf(x),
            "memory": bf(np.random.standard_normal((1, M, C)) * 6.0 / np.sqrt(C)),
            "w2": bf(np.random.standard_normal((F, C)) * 3.0 / np.sqrt(F) / t[:, None]),
            "b2": bf(np.random.standard_normal(C) * 0.5)}


def reference(h, x, memory, w2, b2):
    update_gate = sigmoid((mxq(f64(h), 2, "e4m3") @ mxq(f64(w2), 0, "e4m3")) + f64(b2))
    x_mean = f64(x).mean(axis=1, keepdims=True)
    new_mem = f64(memory) * (1.0 - update_gate) + x_mean * update_gate
    return new_mem.mean(axis=0, keepdims=True)

@@ -1,0 +1,219 @@
+from contextlib import ExitStack
+
+import concourse.mybir as mybir
+from concourse.masks import make_identity
+
+BF16 = mybir.dt.bfloat16
+F32 = mybir.dt.float32
+U32 = mybir.dt.uint32
+U8 = mybir.dt.uint8
+FP8X4 = mybir.dt.float8_e4m3fn_x4
+SIGMOID = mybir.ActivationFunctionType.Sigmoid
+
+P = 128
+PACK = 4
+K_PASS = P * PACK
+
+BATCH, TOKENS, CHANNELS, HIDDEN = 4, 128, 512, 16384
+PASSES = HIDDEN // K_PASS
+
+CHUNK_PASSES = 4
+CHUNK = CHUNK_PASSES * K_PASS
+PAIR = 2
+RUNS = (HIDDEN // CHUNK) * (BATCH // PAIR)
+WORDS_PER_BANK = 512
+PASSES_PER_BANK = 2
+
+STEP_PASSES = 2
+STEPS = PASSES // STEP_PASSES
+LEAD = 2
+H_AHEAD = 3
+W_AHEAD = 3
+
+VECTOR_COLS = 320
+
+FLOPS = 2 * BATCH * TOKENS * HIDDEN * CHANNELS
+
+
+def tile_dynamicmemorybank_pb_k_kernel(tc, h, x, memory, w2, b2, out):
+    nc = tc.nc
+    with ExitStack() as ctx:
+        consts = ctx.enter_context(tc.tile_pool(name="consts", bufs=1))
+        h_raw_pool = ctx.enter_context(tc.tile_pool(name="h_raw", bufs=H_AHEAD * PAIR))
+        w_raw_pool = ctx.enter_context(tc.tile_pool(name="w_raw", bufs=W_AHEAD * STEP_PASSES))
+        grouped_pool = ctx.enter_context(tc.tile_pool(name="grouped", bufs=3))
+        h_mx_pool = ctx.enter_context(tc.tile_pool(name="h_mx", bufs=5))
+        w_mx_pool = ctx.enter_context(tc.tile_pool(name="w_mx", bufs=4))
+        blend_pool = ctx.enter_context(tc.tile_pool(name="blend", bufs=1))
+        acc_pool = ctx.enter_context(tc.psum_pool(name="acc", bufs=1))
+        bank_pool = ctx.enter_context(tc.psum_pool(name="bank", bufs=4))
+        ctx.enter_context(tc.manual_schedule())
+
+        h_raw = {}
+        w_raw = {}
+        h_mx = {}
+        w_mx = {}
+
+        def load_h(run):
+            chunk, pair = divmod(run, BATCH // PAIR)
+            for i in range(PAIR):
+                piece = h_raw_pool.tile([P, CHUNK], BF16, tag="h_raw")
+                nc.sync.dma_start(
+                    out=piece[:], in_=h[pair * PAIR + i, :, chunk * CHUNK : (chunk + 1) * CHUNK]
+                )
+                h_raw[(run, i)] = piece
+
+        def load_w(w_pass):
+            rows = w2[w_pass * K_PASS : (w_pass + 1) * K_PASS, :]
+            raw = w_raw_pool.tile([P, PACK, CHANNELS], BF16, tag="w_raw")
+            nc.sync.dma_start(
+                out=raw[:].rearrange("p (u e) c -> p u e c", u=2),
+                in_=rows.rearrange("(u p e) c -> p u e c", u=2, p=P, e=2),
+            )
+            w_raw[w_pass] = raw
+
+        def transpose_run(run):
+            banks = []
+            for i in range(PAIR):
+                words = h_raw[(run, i)][:].bitcast(F32)
+                for half in range(CHUNK_PASSES // PASSES_PER_BANK):
+                    bank = bank_pool.tile([P, WORDS_PER_BANK // P, P], F32, tag="bank")
+                    for slot in range(WORDS_PER_BANK // P):
+                        first = half * WORDS_PER_BANK + slot * P
+                        nc.tensor.transpose(bank[:, slot, :], words[:, first : first + P], identity[:])
+                    banks.append(bank)
+            return banks
+
+        def copy_out_run(banks):
+            grouped = grouped_pool.tile([P, PAIR * CHUNK_PASSES * TOKENS * PACK], BF16, tag="h_grouped", align_bytes=64)
+            by_bank = grouped[:].bitcast(F32).rearrange(
+                "p (n g r u) -> p n g r u", n=len(banks), g=PASSES_PER_BANK, r=TOKENS, u=2
+            )
+            for n, bank in enumerate(banks):
+                nc.scalar.copy(
+                    out=by_bank[:, n],
+                    in_=bank[:].rearrange("p (g u) r -> p g r u", u=2),
+                )
+            return grouped
+
+        def quantise_h(run, grouped):
+            words = h_mx_pool.tile([P, PAIR * CHUNK_PASSES * TOKENS], U32, tag="h_words", align_bytes=64)
+            scales = h_mx_pool.tile([P, PAIR * CHUNK_PASSES * TOKENS], U8, tag="h_scales", align_bytes=64)
+            nc.vector.quantize_mx(out=words[:].bitcast(FP8X4), scales=scales[:], in_=grouped[:])
+            h_mx[run] = (words, scales)
+
+        def regroup_w(w_pass):
+            raw = w_raw[w_pass]
+            grouped = grouped_pool.tile([P, CHANNELS, PACK], BF16, tag="w_grouped", align_bytes=64)
+            nc.vector.tensor_copy(
+                out=grouped[:, :VECTOR_COLS, :].rearrange("p (c i) t -> p c t i", i=4),
+                in_=raw[:, :, :VECTOR_COLS].rearrange("p t (c i) -> p c t i", i=4),
+            )
+            nc.scalar.copy(
+                out=grouped[:, VECTOR_COLS:, :].rearrange("p (c i) t -> p c t i", i=4),
+                in_=raw[:, :, VECTOR_COLS:].rearrange("p t (c i) -> p c t i", i=4),
+            )
+            return grouped
+
+        def quantise_w(w_pass, grouped):
+            words = w_mx_pool.tile([P, CHANNELS], U32, tag="w_words", align_bytes=64)
+            scales = w_mx_pool.tile([P, CHANNELS], U8, tag="w_scales", align_bytes=64)
+            nc.vector.quantize_mx(
+                out=words[:].bitcast(FP8X4),
+                scales=scales[:],
+                in_=grouped[:].rearrange("p c t -> p (c t)"),
+            )
+            w_mx[w_pass] = (words, scales)
+
+        def multiply(w_pass):
+            chunk, g = divmod(w_pass, CHUNK_PASSES)
+            w_words, w_scales = w_mx[w_pass]
+            for b in range(BATCH):
+                pair, i = divmod(b, PAIR)
+                h_words, h_scales = h_mx[chunk * (BATCH // PAIR) + pair]
+                first = (i * CHUNK_PASSES + g) * TOKENS
+                nc.tensor.matmul_mx(
+                    out=acc[b][:],
+                    lhsT=h_words[:, first : first + TOKENS].bitcast(FP8X4),
+                    lhsT_scale=h_scales[:, first : first + TOKENS],
+                    rhs=w_words[:].bitcast(FP8X4),
+                    rhs_scale=w_scales[:],
+                    start=(w_pass == 0),
+                    stop=(w_pass == PASSES - 1),
+                )
+
+        identity = consts.tile([P, P], F32)
+        make_identity(nc, identity[:])
+        warm = consts.tile([P, 2], F32)
+        nc.vector.memset(warm[:], 0.0)
+        nc.scalar.activation(out=warm[:, 1:2], in_=warm[:, 0:1], func=SIGMOID)
+        ones = consts.tile([P, P], BF16)
+        nc.vector.memset(ones[:], 1.0)
+        mean_quarter = consts.tile([P, P], BF16)
+        nc.vector.memset(mean_quarter[:], 1.0 / (TOKENS * BATCH))
+        b2_rows = consts.tile([P, CHANNELS], BF16)
+        nc.vector.memset(b2_rows[:], 0.0)
+
+        acc = [acc_pool.tile([P, CHANNELS], F32, name="acc%d" % b) for b in range(BATCH)]
+
+        x_sb = consts.tile([P, BATCH, CHANNELS], BF16)
+        nc.sync.dma_start(out=x_sb[:], in_=x.rearrange("b t c -> t b c"))
+        mem_bf = consts.tile([P, CHANNELS], BF16)
+        nc.sync.dma_start(out=mem_bf[:], in_=memory[0])
+        nc.sync.dma_start(out=b2_rows[0:1, :], in_=b2.rearrange("(o c) -> o c", o=1))
+        for run in range(H_AHEAD):
+            load_h(run)
+        for w_pass in range(STEP_PASSES):
+            load_w(w_pass)
+
+        mem_f32 = blend_pool.tile([P, CHANNELS], F32)
+        nc.vector.tensor_copy(out=mem_f32[:], in_=mem_bf[:])
+        mem_quarter = blend_pool.tile([P, CHANNELS], F32)
+        nc.vector.tensor_scalar_mul(out=mem_quarter[:], in0=mem_bf[:], scalar1=1.0 / BATCH)
+        slope = []
+        for b in range(BATCH):
+            mean_bank = bank_pool.tile([P, CHANNELS], F32, tag="bank")
+            nc.tensor.matmul(mean_bank[:], lhsT=mean_quarter[:], rhs=x_sb[:, b, :], start=True, stop=True)
+            slope_b = blend_pool.tile([P, CHANNELS], F32, name="slope%d" % b)
+            nc.vector.tensor_sub(out=slope_b[:], in0=mean_bank[:], in1=mem_quarter[:])
+            slope.append(slope_b)
+        bias_bank = bank_pool.tile([P, CHANNELS], F32, tag="bank")
+        nc.tensor.matmul(bias_bank[:], lhsT=ones[:], rhs=b2_rows[:], start=True, stop=True)
+        bias = blend_pool.tile([P, CHANNELS], F32)
+        nc.scalar.copy(out=bias[:], in_=bias_bank[:])
+
+        for step in range(-LEAD, STEPS):
+            run = step + LEAD
+            if run < RUNS:
+                banks = transpose_run(run)
+                if run + H_AHEAD < RUNS:
+                    load_h(run + H_AHEAD)
+            if step >= 0:
+                passes = range(step * STEP_PASSES, (step + 1) * STEP_PASSES)
+                w_grouped = [regroup_w(w_pass) for w_pass in passes]
+            for w_pass in range((step + W_AHEAD) * STEP_PASSES, (step + W_AHEAD + 1) * STEP_PASSES):
+                if STEP_PASSES <= w_pass < PASSES:
+                    load_w(w_pass)
+            if step >= 0:
+                for w_pass, grouped in zip(passes, w_grouped):
+                    quantise_w(w_pass, grouped)
+                for w_pass in passes:
+                    multiply(w_pass)
+            if run < RUNS:
+                quantise_h(run, copy_out_run(banks))
+
+        gates = []
+        for b in range(BATCH):
+            logit = blend_pool.tile([P, CHANNELS], F32, name="logit%d" % b)
+            nc.vector.tensor_add(out=logit[:], in0=acc[b][:], in1=bias[:])
+            gate = blend_pool.tile([P, CHANNELS], F32, name="gate%d" % b)
+            nc.scalar.activation(out=gate[:], in_=logit[:], func=SIGMOID)
+            gates.append(gate)
+        total = mem_f32
+        for b in range(BATCH):
+            term = blend_pool.tile([P, CHANNELS], F32, name="term%d" % b)
+            nc.vector.tensor_mul(out=term[:], in0=gates[b][:], in1=slope[b][:])
+            new_total = blend_pool.tile([P, CHANNELS], F32, name="total%d" % b)
+            nc.vector.tensor_add(out=new_total[:], in0=total[:], in1=term[:])
+            total = new_total
+        nc.sync.dma_start(out=out[0], in_=total[:])

@@ -19,16 +19,18 @@ PASSES = HIDDEN // K_PASS
 
 CHUNK_PASSES = 4
 CHUNK = CHUNK_PASSES * K_PASS
-PAIR = 2
-RUNS = (HIDDEN // CHUNK) * (BATCH // PAIR)
+PAIR = 1
+RUNS_PER_CHUNK = BATCH // PAIR
+RUNS = (HIDDEN // CHUNK) * RUNS_PER_CHUNK
 WORDS_PER_BANK = 512
 PASSES_PER_BANK = 2
 
-STEP_PASSES = 2
+STEP_PASSES = CHUNK_PASSES // RUNS_PER_CHUNK
 STEPS = PASSES // STEP_PASSES
-LEAD = 2
-H_AHEAD = 3
-W_AHEAD = 3
+LEAD = RUNS_PER_CHUNK
+RAW_BUFS = 6
+H_AHEAD = RAW_BUFS // PAIR
+W_AHEAD = RAW_BUFS // STEP_PASSES
 
 VECTOR_COLS = 320
 
@@ -39,10 +41,10 @@ def tile_dynamicmemorybank_pb_k_kernel(tc, h, x, memory, w2, b2, out):
     nc = tc.nc
     with ExitStack() as ctx:
         consts = ctx.enter_context(tc.tile_pool(name="consts", bufs=1))
-        h_raw_pool = ctx.enter_context(tc.tile_pool(name="h_raw", bufs=H_AHEAD * PAIR))
-        w_raw_pool = ctx.enter_context(tc.tile_pool(name="w_raw", bufs=W_AHEAD * STEP_PASSES))
+        h_raw_pool = ctx.enter_context(tc.tile_pool(name="h_raw", bufs=RAW_BUFS))
+        w_raw_pool = ctx.enter_context(tc.tile_pool(name="w_raw", bufs=RAW_BUFS))
         grouped_pool = ctx.enter_context(tc.tile_pool(name="grouped", bufs=3))
-        h_mx_pool = ctx.enter_context(tc.tile_pool(name="h_mx", bufs=5))
+        h_mx_pool = ctx.enter_context(tc.tile_pool(name="h_mx", bufs=2 * RUNS_PER_CHUNK + 1))
         w_mx_pool = ctx.enter_context(tc.tile_pool(name="w_mx", bufs=4))
         blend_pool = ctx.enter_context(tc.tile_pool(name="blend", bufs=1))
         acc_pool = ctx.enter_context(tc.psum_pool(name="acc", bufs=1))
@@ -55,7 +57,7 @@ def tile_dynamicmemorybank_pb_k_kernel(tc, h, x, memory, w2, b2, out):
         w_mx = {}
 
         def load_h(run):
-            chunk, pair = divmod(run, BATCH // PAIR)
+            chunk, pair = divmod(run, RUNS_PER_CHUNK)
             for i in range(PAIR):
                 piece = h_raw_pool.tile([P, CHUNK], BF16, tag="h_raw")
                 nc.sync.dma_start(
@@ -130,7 +132,7 @@ def tile_dynamicmemorybank_pb_k_kernel(tc, h, x, memory, w2, b2, out):
             w_words, w_scales = w_mx[w_pass]
             for b in range(BATCH):
                 pair, i = divmod(b, PAIR)
-                h_words, h_scales = h_mx[chunk * (BATCH // PAIR) + pair]
+                h_words, h_scales = h_mx[chunk * RUNS_PER_CHUNK + pair]
                 first = (i * CHUNK_PASSES + g) * TOKENS
                 nc.tensor.matmul_mx(
                     out=acc[b][:],
@@ -163,7 +165,8 @@ def tile_dynamicmemorybank_pb_k_kernel(tc, h, x, memory, w2, b2, out):
         nc.sync.dma_start(out=b2_rows[0:1, :], in_=b2.rearrange("(o c) -> o c", o=1))
         for run in range(H_AHEAD):
             load_h(run)
-        for w_pass in range(STEP_PASSES):
+        first_passes = (W_AHEAD - LEAD) * STEP_PASSES
+        for w_pass in range(first_passes):
             load_w(w_pass)
 
         mem_f32 = blend_pool.tile([P, CHANNELS], F32)
@@ -192,7 +195,7 @@ def tile_dynamicmemorybank_pb_k_kernel(tc, h, x, memory, w2, b2, out):
                 passes = range(step * STEP_PASSES, (step + 1) * STEP_PASSES)
                 w_grouped = [regroup_w(w_pass) for w_pass in passes]
             for w_pass in range((step + W_AHEAD) * STEP_PASSES, (step + W_AHEAD + 1) * STEP_PASSES):
-                if STEP_PASSES <= w_pass < PASSES:
+                if w_pass < PASSES:
                     load_w(w_pass)
             if step >= 0:
                 for w_pass, grouped in zip(passes, w_grouped):

@@ -19,7 +19,7 @@ PASSES = HIDDEN // K_PASS
 
 CHUNK_PASSES = 4
 CHUNK = CHUNK_PASSES * K_PASS
-PAIR = 1
+PAIR = 2
 RUNS_PER_CHUNK = BATCH // PAIR
 RUNS = (HIDDEN // CHUNK) * RUNS_PER_CHUNK
 WORDS_PER_BANK = 512
@@ -27,10 +27,8 @@ PASSES_PER_BANK = 2
 
 STEP_PASSES = CHUNK_PASSES // RUNS_PER_CHUNK
 STEPS = PASSES // STEP_PASSES
-LEAD = RUNS_PER_CHUNK
-RAW_BUFS = 6
-H_AHEAD = RAW_BUFS // PAIR
-W_AHEAD = RAW_BUFS // STEP_PASSES
+TRANSPOSE_LEAD = RUNS_PER_CHUNK + 1
+AHEAD = 3
 
 VECTOR_COLS = 320
 
@@ -41,11 +39,11 @@ def tile_dynamicmemorybank_pb_k_kernel(tc, h, x, memory, w2, b2, out):
     nc = tc.nc
     with ExitStack() as ctx:
         consts = ctx.enter_context(tc.tile_pool(name="consts", bufs=1))
-        h_raw_pool = ctx.enter_context(tc.tile_pool(name="h_raw", bufs=RAW_BUFS))
-        w_raw_pool = ctx.enter_context(tc.tile_pool(name="w_raw", bufs=RAW_BUFS))
-        grouped_pool = ctx.enter_context(tc.tile_pool(name="grouped", bufs=3))
+        h_raw_pool = ctx.enter_context(tc.tile_pool(name="h_raw", bufs=AHEAD * PAIR))
+        w_raw_pool = ctx.enter_context(tc.tile_pool(name="w_raw", bufs=AHEAD * STEP_PASSES))
+        grouped_pool = ctx.enter_context(tc.tile_pool(name="grouped", bufs=2 * STEP_PASSES))
         h_mx_pool = ctx.enter_context(tc.tile_pool(name="h_mx", bufs=2 * RUNS_PER_CHUNK + 1))
-        w_mx_pool = ctx.enter_context(tc.tile_pool(name="w_mx", bufs=4))
+        w_mx_pool = ctx.enter_context(tc.tile_pool(name="w_mx", bufs=3 * STEP_PASSES))
         blend_pool = ctx.enter_context(tc.tile_pool(name="blend", bufs=1))
         acc_pool = ctx.enter_context(tc.psum_pool(name="acc", bufs=1))
         bank_pool = ctx.enter_context(tc.psum_pool(name="bank", bufs=4))
@@ -53,8 +51,15 @@ def tile_dynamicmemorybank_pb_k_kernel(tc, h, x, memory, w2, b2, out):
 
         h_raw = {}
         w_raw = {}
+        h_grouped = {}
+        w_grouped = {}
         h_mx = {}
         w_mx = {}
+
+        def step_passes(step):
+            if 0 <= step < STEPS:
+                return range(step * STEP_PASSES, (step + 1) * STEP_PASSES)
+            return range(0)
 
         def load_h(run):
             chunk, pair = divmod(run, RUNS_PER_CHUNK)
@@ -86,7 +91,7 @@ def tile_dynamicmemorybank_pb_k_kernel(tc, h, x, memory, w2, b2, out):
                     banks.append(bank)
             return banks
 
-        def copy_out_run(banks):
+        def copy_out_run(run, banks):
             grouped = grouped_pool.tile([P, PAIR * CHUNK_PASSES * TOKENS * PACK], BF16, tag="h_grouped", align_bytes=64)
             by_bank = grouped[:].bitcast(F32).rearrange(
                 "p (n g r u) -> p n g r u", n=len(banks), g=PASSES_PER_BANK, r=TOKENS, u=2
@@ -96,12 +101,12 @@ def tile_dynamicmemorybank_pb_k_kernel(tc, h, x, memory, w2, b2, out):
                     out=by_bank[:, n],
                     in_=bank[:].rearrange("p (g u) r -> p g r u", u=2),
                 )
-            return grouped
+            h_grouped[run] = grouped
 
-        def quantise_h(run, grouped):
+        def quantise_h(run):
             words = h_mx_pool.tile([P, PAIR * CHUNK_PASSES * TOKENS], U32, tag="h_words", align_bytes=64)
             scales = h_mx_pool.tile([P, PAIR * CHUNK_PASSES * TOKENS], U8, tag="h_scales", align_bytes=64)
-            nc.vector.quantize_mx(out=words[:].bitcast(FP8X4), scales=scales[:], in_=grouped[:])
+            nc.vector.quantize_mx(out=words[:].bitcast(FP8X4), scales=scales[:], in_=h_grouped[run][:])
             h_mx[run] = (words, scales)
 
         def regroup_w(w_pass):
@@ -115,15 +120,15 @@ def tile_dynamicmemorybank_pb_k_kernel(tc, h, x, memory, w2, b2, out):
                 out=grouped[:, VECTOR_COLS:, :].rearrange("p (c i) t -> p c t i", i=4),
                 in_=raw[:, :, VECTOR_COLS:].rearrange("p t (c i) -> p c t i", i=4),
             )
-            return grouped
+            w_grouped[w_pass] = grouped
 
-        def quantise_w(w_pass, grouped):
+        def quantise_w(w_pass):
             words = w_mx_pool.tile([P, CHANNELS], U32, tag="w_words", align_bytes=64)
             scales = w_mx_pool.tile([P, CHANNELS], U8, tag="w_scales", align_bytes=64)
             nc.vector.quantize_mx(
                 out=words[:].bitcast(FP8X4),
                 scales=scales[:],
-                in_=grouped[:].rearrange("p c t -> p (c t)"),
+                in_=w_grouped[w_pass][:].rearrange("p c t -> p (c t)"),
             )
             w_mx[w_pass] = (words, scales)
 
@@ -163,10 +168,9 @@ def tile_dynamicmemorybank_pb_k_kernel(tc, h, x, memory, w2, b2, out):
         mem_bf = consts.tile([P, CHANNELS], BF16)
         nc.sync.dma_start(out=mem_bf[:], in_=memory[0])
         nc.sync.dma_start(out=b2_rows[0:1, :], in_=b2.rearrange("(o c) -> o c", o=1))
-        for run in range(H_AHEAD):
+        for run in range(AHEAD):
             load_h(run)
-        first_passes = (W_AHEAD - LEAD) * STEP_PASSES
-        for w_pass in range(first_passes):
+        for w_pass in step_passes(0):
             load_w(w_pass)
 
         mem_f32 = blend_pool.tile([P, CHANNELS], F32)
@@ -185,25 +189,24 @@ def tile_dynamicmemorybank_pb_k_kernel(tc, h, x, memory, w2, b2, out):
         bias = blend_pool.tile([P, CHANNELS], F32)
         nc.scalar.copy(out=bias[:], in_=bias_bank[:])
 
-        for step in range(-LEAD, STEPS):
-            run = step + LEAD
+        for step in range(-TRANSPOSE_LEAD, STEPS):
+            run = step + TRANSPOSE_LEAD
             if run < RUNS:
                 banks = transpose_run(run)
-                if run + H_AHEAD < RUNS:
-                    load_h(run + H_AHEAD)
-            if step >= 0:
-                passes = range(step * STEP_PASSES, (step + 1) * STEP_PASSES)
-                w_grouped = [regroup_w(w_pass) for w_pass in passes]
-            for w_pass in range((step + W_AHEAD) * STEP_PASSES, (step + W_AHEAD + 1) * STEP_PASSES):
-                if w_pass < PASSES:
-                    load_w(w_pass)
-            if step >= 0:
-                for w_pass, grouped in zip(passes, w_grouped):
-                    quantise_w(w_pass, grouped)
-                for w_pass in passes:
-                    multiply(w_pass)
+                if run + AHEAD < RUNS:
+                    load_h(run + AHEAD)
+            for w_pass in step_passes(step):
+                quantise_w(w_pass)
+            for w_pass in step_passes(step):
+                multiply(w_pass)
+            for w_pass in step_passes(step + 1):
+                regroup_w(w_pass)
+            for w_pass in step_passes(step + 1 + AHEAD):
+                load_w(w_pass)
             if run < RUNS:
-                quantise_h(run, copy_out_run(banks))
+                copy_out_run(run, banks)
+            if 0 <= run - 1 < RUNS:
+                quantise_h(run - 1)
 
         gates = []
         for b in range(BATCH):

from contextlib import ExitStack

import concourse.mybir as mybir
from concourse.masks import make_identity

BF16 = mybir.dt.bfloat16
F32 = mybir.dt.float32
U32 = mybir.dt.uint32
U8 = mybir.dt.uint8
FP8X4 = mybir.dt.float8_e4m3fn_x4
SIGMOID = mybir.ActivationFunctionType.Sigmoid

P = 128
PACK = 4
K_PASS = P * PACK

BATCH, TOKENS, CHANNELS, HIDDEN = 4, 128, 512, 16384
PASSES = HIDDEN // K_PASS

CHUNK_PASSES = 4
CHUNK = CHUNK_PASSES * K_PASS
PAIR = 2
RUNS_PER_CHUNK = BATCH // PAIR
RUNS = (HIDDEN // CHUNK) * RUNS_PER_CHUNK
WORDS_PER_BANK = 512
PASSES_PER_BANK = 2

STEP_PASSES = CHUNK_PASSES // RUNS_PER_CHUNK
STEPS = PASSES // STEP_PASSES
TRANSPOSE_LEAD = RUNS_PER_CHUNK + 1
AHEAD = 3

VECTOR_COLS = 320

FLOPS = 2 * BATCH * TOKENS * HIDDEN * CHANNELS


def tile_dynamicmemorybank_pb_k_kernel(tc, h, x, memory, w2, b2, out):
    nc = tc.nc
    with ExitStack() as ctx:
        consts = ctx.enter_context(tc.tile_pool(name="consts", bufs=1))
        h_raw_pool = ctx.enter_context(tc.tile_pool(name="h_raw", bufs=AHEAD * PAIR))
        w_raw_pool = ctx.enter_context(tc.tile_pool(name="w_raw", bufs=AHEAD * STEP_PASSES))
        grouped_pool = ctx.enter_context(tc.tile_pool(name="grouped", bufs=2 * STEP_PASSES))
        h_mx_pool = ctx.enter_context(tc.tile_pool(name="h_mx", bufs=2 * RUNS_PER_CHUNK + 1))
        w_mx_pool = ctx.enter_context(tc.tile_pool(name="w_mx", bufs=3 * STEP_PASSES))
        blend_pool = ctx.enter_context(tc.tile_pool(name="blend", bufs=1))
        acc_pool = ctx.enter_context(tc.psum_pool(name="acc", bufs=1))
        bank_pool = ctx.enter_context(tc.psum_pool(name="bank", bufs=4))
        ctx.enter_context(tc.manual_schedule())

        h_raw = {}
        w_raw = {}
        h_grouped = {}
        w_grouped = {}
        h_mx = {}
        w_mx = {}

        def step_passes(step):
            if 0 <= step < STEPS:
                return range(step * STEP_PASSES, (step + 1) * STEP_PASSES)
            return range(0)

        def load_h(run):
            chunk, pair = divmod(run, RUNS_PER_CHUNK)
            for i in range(PAIR):
                piece = h_raw_pool.tile([P, CHUNK], BF16, tag="h_raw")
                nc.sync.dma_start(
                    out=piece[:], in_=h[pair * PAIR + i, :, chunk * CHUNK : (chunk + 1) * CHUNK]
                )
                h_raw[(run, i)] = piece

        def load_w(w_pass):
            rows = w2[w_pass * K_PASS : (w_pass + 1) * K_PASS, :]
            raw = w_raw_pool.tile([P, PACK, CHANNELS], BF16, tag="w_raw")
            nc.sync.dma_start(
                out=raw[:].rearrange("p (u e) c -> p u e c", u=2),
                in_=rows.rearrange("(u p e) c -> p u e c", u=2, p=P, e=2),
            )
            w_raw[w_pass] = raw

        def transpose_run(run):
            banks = []
            for i in range(PAIR):
                words = h_raw[(run, i)][:].bitcast(F32)
                for half in range(CHUNK_PASSES // PASSES_PER_BANK):
                    bank = bank_pool.tile([P, WORDS_PER_BANK // P, P], F32, tag="bank")
                    for slot in range(WORDS_PER_BANK // P):
                        first = half * WORDS_PER_BANK + slot * P
                        nc.tensor.transpose(bank[:, slot, :], words[:, first : first + P], identity[:])
                    banks.append(bank)
            return banks

        def copy_out_run(run, banks):
            grouped = grouped_pool.tile([P, PAIR * CHUNK_PASSES * TOKENS * PACK], BF16, tag="h_grouped", align_bytes=64)
            by_bank = grouped[:].bitcast(F32).rearrange(
                "p (n g r u) -> p n g r u", n=len(banks), g=PASSES_PER_BANK, r=TOKENS, u=2
            )
            for n, bank in enumerate(banks):
                nc.scalar.copy(
                    out=by_bank[:, n],
                    in_=bank[:].rearrange("p (g u) r -> p g r u", u=2),
                )
            h_grouped[run] = grouped

        def quantise_h(run):
            words = h_mx_pool.tile([P, PAIR * CHUNK_PASSES * TOKENS], U32, tag="h_words", align_bytes=64)
            scales = h_mx_pool.tile([P, PAIR * CHUNK_PASSES * TOKENS], U8, tag="h_scales", align_bytes=64)
            nc.vector.quantize_mx(out=words[:].bitcast(FP8X4), scales=scales[:], in_=h_grouped[run][:])
            h_mx[run] = (words, scales)

        def regroup_w(w_pass):
            raw = w_raw[w_pass]
            grouped = grouped_pool.tile([P, CHANNELS, PACK], BF16, tag="w_grouped", align_bytes=64)
            nc.vector.tensor_copy(
                out=grouped[:, :VECTOR_COLS, :].rearrange("p (c i) t -> p c t i", i=4),
                in_=raw[:, :, :VECTOR_COLS].rearrange("p t (c i) -> p c t i", i=4),
            )
            nc.scalar.copy(
                out=grouped[:, VECTOR_COLS:, :].rearrange("p (c i) t -> p c t i", i=4),
                in_=raw[:, :, VECTOR_COLS:].rearrange("p t (c i) -> p c t i", i=4),
            )
            w_grouped[w_pass] = grouped

        def quantise_w(w_pass):
            words = w_mx_pool.tile([P, CHANNELS], U32, tag="w_words", align_bytes=64)
            scales = w_mx_pool.tile([P, CHANNELS], U8, tag="w_scales", align_bytes=64)
            nc.vector.quantize_mx(
                out=words[:].bitcast(FP8X4),
                scales=scales[:],
                in_=w_grouped[w_pass][:].rearrange("p c t -> p (c t)"),
            )
            w_mx[w_pass] = (words, scales)

        def multiply(w_pass):
            chunk, g = divmod(w_pass, CHUNK_PASSES)
            w_words, w_scales = w_mx[w_pass]
            for b in range(BATCH):
                pair, i = divmod(b, PAIR)
                h_words, h_scales = h_mx[chunk * RUNS_PER_CHUNK + pair]
                first = (i * CHUNK_PASSES + g) * TOKENS
                nc.tensor.matmul_mx(
                    out=acc[b][:],
                    lhsT=h_words[:, first : first + TOKENS].bitcast(FP8X4),
                    lhsT_scale=h_scales[:, first : first + TOKENS],
                    rhs=w_words[:].bitcast(FP8X4),
                    rhs_scale=w_scales[:],
                    start=(w_pass == 0),
                    stop=(w_pass == PASSES - 1),
                )

        identity = consts.tile([P, P], F32)
        make_identity(nc, identity[:])
        warm = consts.tile([P, 2], F32)
        nc.vector.memset(warm[:], 0.0)
        nc.scalar.activation(out=warm[:, 1:2], in_=warm[:, 0:1], func=SIGMOID)
        ones = consts.tile([P, P], BF16)
        nc.vector.memset(ones[:], 1.0)
        mean_quarter = consts.tile([P, P], BF16)
        nc.vector.memset(mean_quarter[:], 1.0 / (TOKENS * BATCH))
        b2_rows = consts.tile([P, CHANNELS], BF16)
        nc.vector.memset(b2_rows[:], 0.0)

        acc = [acc_pool.tile([P, CHANNELS], F32, name="acc%d" % b) for b in range(BATCH)]

        x_sb = consts.tile([P, BATCH, CHANNELS], BF16)
        nc.sync.dma_start(out=x_sb[:], in_=x.rearrange("b t c -> t b c"))
        mem_bf = consts.tile([P, CHANNELS], BF16)
        nc.sync.dma_start(out=mem_bf[:], in_=memory[0])
        nc.sync.dma_start(out=b2_rows[0:1, :], in_=b2.rearrange("(o c) -> o c", o=1))
        for run in range(AHEAD):
            load_h(run)
        for w_pass in step_passes(0):
            load_w(w_pass)

        mem_f32 = blend_pool.tile([P, CHANNELS], F32)
        nc.vector.tensor_copy(out=mem_f32[:], in_=mem_bf[:])
        mem_quarter = blend_pool.tile([P, CHANNELS], F32)
        nc.vector.tensor_scalar_mul(out=mem_quarter[:], in0=mem_bf[:], scalar1=1.0 / BATCH)
        slope = []
        for b in range(BATCH):
            mean_bank = bank_pool.tile([P, CHANNELS], F32, tag="bank")
            nc.tensor.matmul(mean_bank[:], lhsT=mean_quarter[:], rhs=x_sb[:, b, :], start=True, stop=True)
            slope_b = blend_pool.tile([P, CHANNELS], F32, name="slope%d" % b)
            nc.vector.tensor_sub(out=slope_b[:], in0=mean_bank[:], in1=mem_quarter[:])
            slope.append(slope_b)
        bias_bank = bank_pool.tile([P, CHANNELS], F32, tag="bank")
        nc.tensor.matmul(bias_bank[:], lhsT=ones[:], rhs=b2_rows[:], start=True, stop=True)
        bias = blend_pool.tile([P, CHANNELS], F32)
        nc.scalar.copy(out=bias[:], in_=bias_bank[:])

        for step in range(-TRANSPOSE_LEAD, STEPS):
            run = step + TRANSPOSE_LEAD
            if run < RUNS:
                banks = transpose_run(run)
                if run + AHEAD < RUNS:
                    load_h(run + AHEAD)
            for w_pass in step_passes(step):
                quantise_w(w_pass)
            for w_pass in step_passes(step):
                multiply(w_pass)
            for w_pass in step_passes(step + 1):
                regroup_w(w_pass)
            for w_pass in step_passes(step + 1 + AHEAD):
                load_w(w_pass)
            if run < RUNS:
                copy_out_run(run, banks)
            if 0 <= run - 1 < RUNS:
                quantise_h(run - 1)

        gates = []
        for b in range(BATCH):
            logit = blend_pool.tile([P, CHANNELS], F32, name="logit%d" % b)
            nc.vector.tensor_add(out=logit[:], in0=acc[b][:], in1=bias[:])
            gate = blend_pool.tile([P, CHANNELS], F32, name="gate%d" % b)
            nc.scalar.activation(out=gate[:], in_=logit[:], func=SIGMOID)
            gates.append(gate)
        total = mem_f32
        for b in range(BATCH):
            term = blend_pool.tile([P, CHANNELS], F32, name="term%d" % b)
            nc.vector.tensor_mul(out=term[:], in0=gates[b][:], in1=slope[b][:])
            new_total = blend_pool.tile([P, CHANNELS], F32, name="total%d" % b)
            nc.vector.tensor_add(out=new_total[:], in0=total[:], in1=term[:])
            total = new_total
        nc.sync.dma_start(out=out[0], in_=total[:])
